import numpy as np
import ml_dtypes


def mxq(x, axis, fmt="e4m3"):
    dtype, down = {"e4m3": (ml_dtypes.float8_e4m3fn, 7), "e5m2": (ml_dtypes.float8_e5m2, 14)}[fmt]
    v = np.moveaxis(np.asarray(x, np.float32).astype(ml_dtypes.bfloat16).astype(np.float64), axis, -1)
    blocks = v.reshape(v.shape[:-1] + (-1, 32))
    amax = np.abs(blocks).max(-1, keepdims=True)
    byte = np.maximum(np.where(amax > 0, np.frexp(amax)[1] - 1 + 127, 0) - down, 1)
    scale = np.exp2(byte - 127.0)
    codes = (blocks / scale).astype(np.float32).astype(dtype).astype(np.float64)
    return np.moveaxis((codes * scale).reshape(v.shape), -1, axis)


WIDE = False


def mx_kscale(k):
    if not WIDE:
        return np.ones(k)
    levels = np.array([10, -10, 5, -5, 0])
    a = np.random.permutation(np.resize(levels, k // 512 * 4)).reshape(k // 512, 4)
    idx = np.arange(k)
    return np.exp2(a[idx // 512, idx % 128 // 32])


BF16 = ml_dtypes.bfloat16


def bf(x):
    return np.asarray(x, np.float32).astype(BF16)


def f64(x):
    return np.asarray(x).astype(np.float64)


B, D_IN, H, D_OUT, DEPTH, Q = 8192, 1024, 512, 1024, 3, 2


def quantum_probs(qw):
    n = qw.shape[1]
    s0r, s0i, s1r, s1i = np.ones(n), np.zeros(n), np.zeros(n), np.zeros(n)
    for d in range(qw.shape[0]):
        th = qw[d, :, 0, 0]
        ph = qw[d, :, 1, 1]
        c, s = np.cos(th), np.sin(th)
        n0r, n0i = c * s0r - s * s1r, c * s0i - s * s1i
        n1r, n1i = s * s0r + c * s1r, s * s0i + c * s1i
        cp, sp = np.cos(ph), np.sin(ph)
        s0r, s0i = n0r, n0i
        s1r, s1i = n1r * cp - n1i * sp, n1r * sp + n1i * cp
    return s0r * s0r + s0i * s0i


def setup_inputs():
    s, t = mx_kscale(H), mx_kscale(H)
    return {"h0": bf(np.maximum(np.random.standard_normal((B, H)), 0.0) * s),
            "w1": bf(np.random.standard_normal((H, H)) * 1.4 / np.sqrt(H) / s[:, None] * t),
            "b1": bf(np.random.standard_normal(H) * 0.3 * t),
            "q1_qw": bf(np.random.standard_normal((DEPTH, H, Q, Q))),
            "q1_cw": bf(np.random.standard_normal((H, H)) * 1.4 / np.sqrt(H) / t[:, None]),
            "q1_cb": bf(np.random.standard_normal(H) * 0.3)}


def reference(h0, w1, b1, q1_qw, q1_cw, q1_cb):
    h1 = np.maximum((mxq(f64(h0), 1, "e4m3") @ mxq(f64(w1), 0, "e4m3")) + f64(b1), 0.0)
    return np.tanh((mxq(h1, 1, "e4m3") @ mxq(f64(q1_cw), 0, "e4m3")) + f64(q1_cb) + quantum_probs(f64(q1_qw))[None, :])

@@ -1,0 +1,210 @@
+import math
+from contextlib import ExitStack
+
+import concourse.mybir as mybir
+from concourse.masks import make_identity
+
+F32 = mybir.dt.float32
+BF16 = mybir.dt.bfloat16
+U32 = mybir.dt.uint32
+U8 = mybir.dt.uint8
+FP8X4 = mybir.dt.float8_e4m3fn_x4
+ACT = mybir.ActivationFunctionType
+ALU = mybir.AluOpType
+
+P = 128
+PACK = 4
+BATCH = 8192
+H = P * PACK
+DEPTH = 3
+ROWS = 512
+SUB = ROWS // P
+ROUNDS = BATCH // ROWS
+ROUND_TO_INT = 1.5 * 2.0**23
+
+FLOPS = 2 * 2 * BATCH * H * H
+
+
+def quantise(nc, pool, grouped, name):
+    columns = grouped.shape[1] // PACK
+    words = pool.tile([P, columns], U32, name=name + "_words", align_bytes=64)
+    scales = pool.tile([P, columns], U8, name=name + "_scales", align_bytes=64)
+    nc.vector.quantize_mx(out=words[:].bitcast(FP8X4), scales=scales[:], in_=grouped)
+    return words, scales
+
+
+def output_bias(nc, small, keep, psum, ident, q1_qw, q1_cb):
+    angles = small.tile([P, DEPTH, PACK * 4], BF16, name="angles")
+    nc.scalar.dma_start(out=angles[:], in_=q1_qw.rearrange("d (q i) a b -> q d (i a b)", i=PACK))
+    cb = small.tile([P, PACK], BF16, name="cb")
+    nc.scalar.dma_start(out=cb[:], in_=q1_cb.rearrange("(q i) -> q i", i=PACK))
+
+    diagonal = angles[:].rearrange("q d (i e) -> q (d i) e", e=4)[:, :, 0:4:3]
+    turns = small.tile([P, 2, DEPTH * PACK, 2], F32, name="turns")
+    nc.vector.tensor_scalar(
+        out=turns[:, 0], in0=diagonal, scalar1=0.5 / math.pi, scalar2=0.0, op0=ALU.mult, op1=ALU.add
+    )
+    nc.vector.tensor_scalar(
+        out=turns[:, 1], in0=diagonal, scalar1=0.5 / math.pi, scalar2=0.25, op0=ALU.mult, op1=ALU.add
+    )
+    whole = small.tile([P, 2, DEPTH * PACK, 2], F32, name="whole")
+    nc.vector.tensor_scalar(
+        out=whole[:], in0=turns[:], scalar1=ROUND_TO_INT, scalar2=ROUND_TO_INT, op0=ALU.add, op1=ALU.subtract
+    )
+    part = small.tile([P, 2, DEPTH * PACK, 2], F32, name="part")
+    nc.vector.tensor_tensor(out=part[:], in0=turns[:], in1=whole[:], op=ALU.subtract)
+    trig = small.tile([P, 2, DEPTH * PACK, 2], F32, name="trig")
+    nc.scalar.activation(out=trig[:], in_=part[:], func=ACT.Sin, scale=2.0 * math.pi)
+
+    def both(kind, d, angle):
+        column = trig[:, kind, d * PACK : (d + 1) * PACK, angle]
+        return column.unsqueeze(1).to_broadcast([P, 2, PACK])
+
+    a0 = small.tile([P, 2, PACK], F32, name="a0_start")
+    a1 = small.tile([P, 2, PACK], F32, name="a1_start")
+    nc.gpsimd.memset(a0[:], 0.0)
+    nc.gpsimd.memset(a0[:, 0, :], 1.0)
+    nc.gpsimd.memset(a1[:], 0.0)
+    for d in range(DEPTH):
+        cos_a0 = small.tile([P, 2, PACK], F32)
+        sin_a1 = small.tile([P, 2, PACK], F32)
+        new_a0 = small.tile([P, 2, PACK], F32)
+        nc.gpsimd.tensor_tensor(out=cos_a0[:], in0=a0[:], in1=both(1, d, 0), op=ALU.mult)
+        nc.gpsimd.tensor_tensor(out=sin_a1[:], in0=a1[:], in1=both(0, d, 0), op=ALU.mult)
+        nc.gpsimd.tensor_tensor(out=new_a0[:], in0=cos_a0[:], in1=sin_a1[:], op=ALU.subtract)
+        if d < DEPTH - 1:
+            sin_a0 = small.tile([P, 2, PACK], F32)
+            cos_a1 = small.tile([P, 2, PACK], F32)
+            turned = small.tile([P, 2, PACK], F32)
+            nc.gpsimd.tensor_tensor(out=sin_a0[:], in0=a0[:], in1=both(0, d, 0), op=ALU.mult)
+            nc.gpsimd.tensor_tensor(out=cos_a1[:], in0=a1[:], in1=both(1, d, 0), op=ALU.mult)
+            nc.gpsimd.tensor_tensor(out=turned[:], in0=sin_a0[:], in1=cos_a1[:], op=ALU.add)
+            by_cos = small.tile([P, 2, PACK], F32)
+            by_sin = small.tile([P, 2, PACK], F32)
+            new_a1 = small.tile([P, 2, PACK], F32)
+            nc.gpsimd.tensor_tensor(out=by_cos[:], in0=turned[:], in1=both(1, d, 1), op=ALU.mult)
+            nc.gpsimd.tensor_tensor(out=by_sin[:], in0=turned[:], in1=both(0, d, 1), op=ALU.mult)
+            nc.gpsimd.tensor_tensor(out=new_a1[:, 0, :], in0=by_cos[:, 0, :], in1=by_sin[:, 1, :], op=ALU.subtract)
+            nc.gpsimd.tensor_tensor(out=new_a1[:, 1, :], in0=by_sin[:, 0, :], in1=by_cos[:, 1, :], op=ALU.add)
+            a1 = new_a1
+        a0 = new_a0
+    squares = small.tile([P, 2, PACK], F32, name="squares")
+    nc.gpsimd.tensor_tensor(out=squares[:], in0=a0[:], in1=a0[:], op=ALU.mult)
+    prob = small.tile([P, PACK], F32, name="prob")
+    nc.gpsimd.tensor_tensor(out=prob[:], in0=squares[:, 0, :], in1=squares[:, 1, :], op=ALU.add)
+    bias_column = small.tile([P, PACK], F32, name="bias_column")
+    nc.gpsimd.tensor_tensor(out=bias_column[:], in0=prob[:], in1=cb[:], op=ALU.add)
+
+    repeated = small.tile([P, PACK, P], F32, name="repeated")
+    nc.vector.tensor_copy(out=repeated[:], in_=bias_column[:].unsqueeze(2).to_broadcast([P, PACK, P]))
+    spread = psum.tile([P, PACK, P], F32, name="spread", tag="product2")
+    for i in range(PACK):
+        nc.tensor.transpose(out=spread[:, i, :], in_=repeated[:, i, :], identity=ident[:])
+    bias_row = keep.tile([P, H], F32, name="bias_row")
+    nc.vector.tensor_copy(
+        out=bias_row[:].rearrange("p (q i) -> p q i", i=PACK), in_=spread[:].rearrange("p i q -> p q i")
+    )
+    return bias_row
+
+
+def tile_quantumneuralnetwork_pa_t_kernel(tc, h0, w1, b1, q1_qw, q1_cw, q1_cb, out):
+    nc = tc.nc
+    with ExitStack() as ctx:
+        keep = ctx.enter_context(tc.tile_pool(name="keep", bufs=1))
+        small = ctx.enter_context(tc.tile_pool(name="small", bufs=2))
+        rows_in = ctx.enter_context(tc.tile_pool(name="rows_in", bufs=ROUNDS))
+        work = ctx.enter_context(tc.tile_pool(name="work", bufs=3))
+        rows_out = ctx.enter_context(tc.tile_pool(name="rows_out", bufs=4))
+        psum_t = ctx.enter_context(tc.psum_pool(name="psum_t", bufs=2))
+        psum_1 = ctx.enter_context(tc.psum_pool(name="psum_1", bufs=3))
+        psum_2 = ctx.enter_context(tc.psum_pool(name="psum_2", bufs=3))
+
+        h0_rounds = h0.rearrange("(g c r) k -> g c (r k)", c=P, r=SUB)
+        out_rounds = out.rearrange("(g c r) n -> g c r n", c=P, r=SUB)
+
+        x_tiles = []
+        for g in range(ROUNDS):
+            x_tiles.append(rows_in.tile([P, SUB * H], BF16, name="x"))
+        nc.sync.dma_start(out=x_tiles[0][:], in_=h0_rounds[0])
+        w1_raw = keep.tile([P, PACK, H], BF16, name="w1_raw")
+        nc.sync.dma_start(
+            out=w1_raw[:].rearrange("q (u e) j -> q u e j", u=2),
+            in_=w1.rearrange("(u q e) j -> q u e j", u=2, e=2),
+        )
+        cw_raw = keep.tile([P, PACK, H], BF16, name="cw_raw")
+        nc.sync.dma_start(out=cw_raw[:], in_=q1_cw.rearrange("(q t) n -> q t n", t=PACK))
+        for g in range(1, ROUNDS):
+            nc.sync.dma_start(out=x_tiles[g][:], in_=h0_rounds[g])
+        b1_raw = small.tile([P, PACK], BF16, name="b1_raw")
+        nc.scalar.dma_start(out=b1_raw[:], in_=b1.rearrange("(q t) -> q t", t=PACK))
+
+        ident = keep.tile([P, P], F32, name="ident")
+        make_identity(nc, ident[:])
+        b1_column = keep.tile([P, PACK], F32, name="b1_column")
+        nc.vector.tensor_copy(out=b1_column[:], in_=b1_raw[:])
+
+        w1_grouped = keep.tile([P, H, PACK], BF16, name="w1_grouped", align_bytes=64)
+        nc.vector.tensor_copy(
+            out=w1_grouped[:].rearrange("q (t m) k -> q t m k", t=PACK),
+            in_=w1_raw[:].rearrange("q k (m t) -> q t m k", t=PACK),
+        )
+        w1_words, w1_scales = quantise(nc, keep, w1_grouped[:].rearrange("q j k -> q (j k)"), "w1")
+        cw_grouped = keep.tile([P, H, PACK], BF16, name="cw_grouped", align_bytes=64)
+        nc.vector.tensor_copy(out=cw_grouped[:], in_=cw_raw[:].rearrange("q t n -> q n t"))
+        cw_words, cw_scales = quantise(nc, keep, cw_grouped[:].rearrange("q n t -> q (n t)"), "cw")
+
+        bias_row = output_bias(nc, small, keep, psum_2, ident, q1_qw, q1_cb)
+
+        for g in range(ROUNDS):
+            x_words = x_tiles[g][:].bitcast(F32)
+            h0_grouped = work.tile([P, ROWS * PACK], BF16, name="h0_grouped", align_bytes=64)
+            h0_pairs = h0_grouped[:].bitcast(F32).rearrange("q (h r c u) -> q h r c u", h=2, r=2, u=2)
+            for half in range(2):
+                flipped = psum_t.tile([P, 2, 2, P], F32, name="flipped")
+                for r in range(2):
+                    for u in range(2):
+                        square = ((2 * half + r) * 2 + u) * P
+                        nc.tensor.transpose(
+                            out=flipped[:, r, u, :], in_=x_words[:, square : square + P], identity=ident[:]
+                        )
+                empty = nc.scalar.copy if half == 0 else nc.vector.tensor_copy
+                empty(out=h0_pairs[:, half], in_=flipped[:].rearrange("q r u c -> q r c u"))
+            h0_words, h0_scales = quantise(nc, work, h0_grouped[:], "h0")
+
+            h1_planes = work.tile([P, PACK, ROWS], BF16, name="h1_planes")
+            for t in range(PACK):
+                product1 = psum_1.tile([P, ROWS], F32, name="product1")
+                nc.tensor.matmul_mx(
+                    out=product1[:],
+                    lhsT=w1_words[:, t * P : (t + 1) * P].bitcast(FP8X4),
+                    lhsT_scale=w1_scales[:, t * P : (t + 1) * P],
+                    rhs=h0_words[:].bitcast(FP8X4),
+                    rhs_scale=h0_scales[:],
+                    start=True,
+                    stop=True,
+                )
+                nc.scalar.activation(
+                    out=h1_planes[:, t, :], in_=product1[:], func=ACT.Relu, bias=b1_column[:, t : t + 1], scale=1.0
+                )
+            h1_grouped = work.tile([P, ROWS, PACK], BF16, name="h1_grouped", align_bytes=64)
+            nc.vector.tensor_copy(
+                out=h1_grouped[:].rearrange("q (c i) t -> q c t i", i=4),
+                in_=h1_planes[:].rearrange("q t (c i) -> q c t i", i=4),
+            )
+            h1_words, h1_scales = quantise(nc, work, h1_grouped[:].rearrange("q c t -> q (c t)"), "h1")
+
+            y = rows_out.tile([P, SUB, H], F32, name="y")
+            for r in range(SUB):
+                product2 = psum_2.tile([P, H], F32, name="product2")
+                nc.tensor.matmul_mx(
+                    out=product2[:],
+                    lhsT=h1_words[:, r * P : (r + 1) * P].bitcast(FP8X4),
+                    lhsT_scale=h1_scales[:, r * P : (r + 1) * P],
+                    rhs=cw_words[:].bitcast(FP8X4),
+                    rhs_scale=cw_scales[:],
+                    start=True,
+                    stop=True,
+                )
+                nc.vector.tensor_tensor(out=y[:, r, :], in0=product2[:], in1=bias_row[:], op=ALU.add)
+            nc.scalar.activation(out=y[:], in_=y[:], func=ACT.Tanh)
+            nc.sync.dma_start(out=out_rounds[g], in_=y[:])

@@ -21,6 +21,14 @@ ROWS = 512
 SUB = ROWS // P
 ROUNDS = BATCH // ROWS
 ROUND_TO_INT = 1.5 * 2.0**23
+COS = 0
+SIN = 1
+THETA = 0
+PHI = 1
+FIRST_LAG = 1
+REGROUP_LAG = 2
+SECOND_LAG = 3
+TANH_LAG = 4
 
 FLOPS = 2 * 2 * BATCH * H * H
 
@@ -33,7 +41,7 @@ def quantise(nc, pool, grouped, name):
     return words, scales
 
 
-def output_bias(nc, small, keep, psum, ident, q1_qw, q1_cb):
+def output_bias_column(nc, small, q1_qw, q1_cb):
     angles = small.tile([P, DEPTH, PACK * 4], BF16, name="angles")
     nc.scalar.dma_start(out=angles[:], in_=q1_qw.rearrange("d (q i) a b -> q d (i a b)", i=PACK))
     cb = small.tile([P, PACK], BF16, name="cb")
@@ -42,10 +50,10 @@ def output_bias(nc, small, keep, psum, ident, q1_qw, q1_cb):
     diagonal = angles[:].rearrange("q d (i e) -> q (d i) e", e=4)[:, :, 0:4:3]
     turns = small.tile([P, 2, DEPTH * PACK, 2], F32, name="turns")
     nc.vector.tensor_scalar(
-        out=turns[:, 0], in0=diagonal, scalar1=0.5 / math.pi, scalar2=0.0, op0=ALU.mult, op1=ALU.add
+        out=turns[:, COS], in0=diagonal, scalar1=0.5 / math.pi, scalar2=0.25, op0=ALU.mult, op1=ALU.add
     )
     nc.vector.tensor_scalar(
-        out=turns[:, 1], in0=diagonal, scalar1=0.5 / math.pi, scalar2=0.25, op0=ALU.mult, op1=ALU.add
+        out=turns[:, SIN], in0=diagonal, scalar1=0.5 / math.pi, scalar2=0.0, op0=ALU.mult, op1=ALU.add
     )
     whole = small.tile([P, 2, DEPTH * PACK, 2], F32, name="whole")
     nc.vector.tensor_scalar(
@@ -56,34 +64,38 @@ def output_bias(nc, small, keep, psum, ident, q1_qw, q1_cb):
     trig = small.tile([P, 2, DEPTH * PACK, 2], F32, name="trig")
     nc.scalar.activation(out=trig[:], in_=part[:], func=ACT.Sin, scale=2.0 * math.pi)
 
-    def both(kind, d, angle):
-        column = trig[:, kind, d * PACK : (d + 1) * PACK, angle]
-        return column.unsqueeze(1).to_broadcast([P, 2, PACK])
+    def layer(d):
+        return slice(d * PACK, (d + 1) * PACK)
 
-    a0 = small.tile([P, 2, PACK], F32, name="a0_start")
-    a1 = small.tile([P, 2, PACK], F32, name="a1_start")
-    nc.gpsimd.memset(a0[:], 0.0)
-    nc.gpsimd.memset(a0[:, 0, :], 1.0)
-    nc.gpsimd.memset(a1[:], 0.0)
-    for d in range(DEPTH):
+    def rotation(kind, d):
+        return trig[:, kind, layer(d), THETA].unsqueeze(1).to_broadcast([P, 2, PACK])
+
+    a0 = small.tile([P, 2, PACK], F32, name="a0_first")
+    nc.gpsimd.memset(a0[:, 1, :], 0.0)
+    nc.gpsimd.tensor_copy(out=a0[:, 0, :], in_=trig[:, COS, layer(0), THETA])
+    a1 = small.tile([P, 2, PACK], F32, name="a1_first")
+    nc.gpsimd.tensor_tensor(out=a1[:], in0=trig[:, :, layer(0), PHI], in1=rotation(SIN, 0), op=ALU.mult)
+    for d in range(1, DEPTH):
         cos_a0 = small.tile([P, 2, PACK], F32)
         sin_a1 = small.tile([P, 2, PACK], F32)
         new_a0 = small.tile([P, 2, PACK], F32)
-        nc.gpsimd.tensor_tensor(out=cos_a0[:], in0=a0[:], in1=both(1, d, 0), op=ALU.mult)
-        nc.gpsimd.tensor_tensor(out=sin_a1[:], in0=a1[:], in1=both(0, d, 0), op=ALU.mult)
+        nc.gpsimd.tensor_tensor(out=cos_a0[:], in0=a0[:], in1=rotation(COS, d), op=ALU.mult)
+        nc.gpsimd.tensor_tensor(out=sin_a1[:], in0=a1[:], in1=rotation(SIN, d), op=ALU.mult)
         nc.gpsimd.tensor_tensor(out=new_a0[:], in0=cos_a0[:], in1=sin_a1[:], op=ALU.subtract)
         if d < DEPTH - 1:
             sin_a0 = small.tile([P, 2, PACK], F32)
             cos_a1 = small.tile([P, 2, PACK], F32)
             turned = small.tile([P, 2, PACK], F32)
-            nc.gpsimd.tensor_tensor(out=sin_a0[:], in0=a0[:], in1=both(0, d, 0), op=ALU.mult)
-            nc.gpsimd.tensor_tensor(out=cos_a1[:], in0=a1[:], in1=both(1, d, 0), op=ALU.mult)
+            nc.gpsimd.tensor_tensor(out=sin_a0[:], in0=a0[:], in1=rotation(SIN, d), op=ALU.mult)
+            nc.gpsimd.tensor_tensor(out=cos_a1[:], in0=a1[:], in1=rotation(COS, d), op=ALU.mult)
             nc.gpsimd.tensor_tensor(out=turned[:], in0=sin_a0[:], in1=cos_a1[:], op=ALU.add)
             by_cos = small.tile([P, 2, PACK], F32)
             by_sin = small.tile([P, 2, PACK], F32)
             new_a1 = small.tile([P, 2, PACK], F32)
-            nc.gpsimd.tensor_tensor(out=by_cos[:], in0=turned[:], in1=both(1, d, 1), op=ALU.mult)
-            nc.gpsimd.tensor_tensor(out=by_sin[:], in0=turned[:], in1=both(0, d, 1), op=ALU.mult)
+            cos_phi = trig[:, COS, layer(d), PHI].unsqueeze(1).to_broadcast([P, 2, PACK])
+            sin_phi = trig[:, SIN, layer(d), PHI].unsqueeze(1).to_broadcast([P, 2, PACK])
+            nc.gpsimd.tensor_tensor(out=by_cos[:], in0=turned[:], in1=cos_phi, op=ALU.mult)
+            nc.gpsimd.tensor_tensor(out=by_sin[:], in0=turned[:], in1=sin_phi, op=ALU.mult)
             nc.gpsimd.tensor_tensor(out=new_a1[:, 0, :], in0=by_cos[:, 0, :], in1=by_sin[:, 1, :], op=ALU.subtract)
             nc.gpsimd.tensor_tensor(out=new_a1[:, 1, :], in0=by_sin[:, 0, :], in1=by_cos[:, 1, :], op=ALU.add)
             a1 = new_a1
@@ -94,22 +106,13 @@ def output_bias(nc, small, keep, psum, ident, q1_qw, q1_cb):
     nc.gpsimd.tensor_tensor(out=prob[:], in0=squares[:, 0, :], in1=squares[:, 1, :], op=ALU.add)
     bias_column = small.tile([P, PACK], F32, name="bias_column")
     nc.gpsimd.tensor_tensor(out=bias_column[:], in0=prob[:], in1=cb[:], op=ALU.add)
-
-    repeated = small.tile([P, PACK, P], F32, name="repeated")
-    nc.vector.tensor_copy(out=repeated[:], in_=bias_column[:].unsqueeze(2).to_broadcast([P, PACK, P]))
-    spread = psum.tile([P, PACK, P], F32, name="spread", tag="product2")
-    for i in range(PACK):
-        nc.tensor.transpose(out=spread[:, i, :], in_=repeated[:, i, :], identity=ident[:])
-    bias_row = keep.tile([P, H], F32, name="bias_row")
-    nc.vector.tensor_copy(
-        out=bias_row[:].rearrange("p (q i) -> p q i", i=PACK), in_=spread[:].rearrange("p i q -> p q i")
-    )
-    return bias_row
+    return bias_column
 
 
 def tile_quantumneuralnetwork_pa_t_kernel(tc, h0, w1, b1, q1_qw, q1_cw, q1_cb, out):
     nc = tc.nc
     with ExitStack() as ctx:
+        ctx.enter_context(tc.manual_schedule())
         keep = ctx.enter_context(tc.tile_pool(name="keep", bufs=1))
         small = ctx.enter_context(tc.tile_pool(name="small", bufs=2))
         rows_in = ctx.enter_context(tc.tile_pool(name="rows_in", bufs=ROUNDS))
@@ -122,24 +125,26 @@ def tile_quantumneuralnetwork_pa_t_kernel(tc, h0, w1, b1, q1_qw, q1_cw, q1_cb, o
         h0_rounds = h0.rearrange("(g c r) k -> g c (r k)", c=P, r=SUB)
         out_rounds = out.rearrange("(g c r) n -> g c r n", c=P, r=SUB)
 
-        x_tiles = []
-        for g in range(ROUNDS):
-            x_tiles.append(rows_in.tile([P, SUB * H], BF16, name="x"))
-        nc.sync.dma_start(out=x_tiles[0][:], in_=h0_rounds[0])
         w1_raw = keep.tile([P, PACK, H], BF16, name="w1_raw")
         nc.sync.dma_start(
             out=w1_raw[:].rearrange("q (u e) j -> q u e j", u=2),
             in_=w1.rearrange("(u q e) j -> q u e j", u=2, e=2),
         )
+        x_tiles = []
+        for g in range(ROUNDS):
+            x_tiles.append(rows_in.tile([P, SUB * H], BF16, name="x"))
+        nc.sync.dma_start(out=x_tiles[0][:], in_=h0_rounds[0])
+        nc.sync.dma_start(out=x_tiles[1][:], in_=h0_rounds[1])
         cw_raw = keep.tile([P, PACK, H], BF16, name="cw_raw")
         nc.sync.dma_start(out=cw_raw[:], in_=q1_cw.rearrange("(q t) n -> q t n", t=PACK))
-        for g in range(1, ROUNDS):
+        for g in range(2, ROUNDS):
             nc.sync.dma_start(out=x_tiles[g][:], in_=h0_rounds[g])
-        b1_raw = small.tile([P, PACK], BF16, name="b1_raw")
-        nc.scalar.dma_start(out=b1_raw[:], in_=b1.rearrange("(q t) -> q t", t=PACK))
 
         ident = keep.tile([P, P], F32, name="ident")
         make_identity(nc, ident[:])
+        b1_raw = small.tile([P, PACK], BF16, name="b1_raw")
+        nc.scalar.dma_start(out=b1_raw[:], in_=b1.rearrange("(q t) -> q t", t=PACK))
+        bias_column = output_bias_column(nc, small, q1_qw, q1_cb)
         b1_column = keep.tile([P, PACK], F32, name="b1_column")
         nc.vector.tensor_copy(out=b1_column[:], in_=b1_raw[:])
 
@@ -149,16 +154,13 @@ def tile_quantumneuralnetwork_pa_t_kernel(tc, h0, w1, b1, q1_qw, q1_cw, q1_cb, o
             in_=w1_raw[:].rearrange("q k (m t) -> q t m k", t=PACK),
         )
         w1_words, w1_scales = quantise(nc, keep, w1_grouped[:].rearrange("q j k -> q (j k)"), "w1")
-        cw_grouped = keep.tile([P, H, PACK], BF16, name="cw_grouped", align_bytes=64)
-        nc.vector.tensor_copy(out=cw_grouped[:], in_=cw_raw[:].rearrange("q t n -> q n t"))
-        cw_words, cw_scales = quantise(nc, keep, cw_grouped[:].rearrange("q n t -> q (n t)"), "cw")
 
-        bias_row = output_bias(nc, small, keep, psum_2, ident, q1_qw, q1_cb)
+        h0_grouped, h0_packed, h1_planes, h1_grouped, h1_packed, results = {}, {}, {}, {}, {}, {}
 
-        for g in range(ROUNDS):
+        def transpose_rows(g):
             x_words = x_tiles[g][:].bitcast(F32)
-            h0_grouped = work.tile([P, ROWS * PACK], BF16, name="h0_grouped", align_bytes=64)
-            h0_pairs = h0_grouped[:].bitcast(F32).rearrange("q (h r c u) -> q h r c u", h=2, r=2, u=2)
+            h0_grouped[g] = work.tile([P, ROWS * PACK], BF16, name="h0_grouped", align_bytes=64)
+            h0_pairs = h0_grouped[g][:].bitcast(F32).rearrange("q (h r c u) -> q h r c u", h=2, r=2, u=2)
             for half in range(2):
                 flipped = psum_t.tile([P, 2, 2, P], F32, name="flipped")
                 for r in range(2):
@@ -169,9 +171,10 @@ def tile_quantumneuralnetwork_pa_t_kernel(tc, h0, w1, b1, q1_qw, q1_cw, q1_cb, o
                         )
                 empty = nc.scalar.copy if half == 0 else nc.vector.tensor_copy
                 empty(out=h0_pairs[:, half], in_=flipped[:].rearrange("q r u c -> q r c u"))
-            h0_words, h0_scales = quantise(nc, work, h0_grouped[:], "h0")
 
-            h1_planes = work.tile([P, PACK, ROWS], BF16, name="h1_planes")
+        def first_product(g):
+            h0_words, h0_scales = h0_packed[g]
+            h1_planes[g] = work.tile([P, PACK, ROWS], BF16, name="h1_planes")
             for t in range(PACK):
                 product1 = psum_1.tile([P, ROWS], F32, name="product1")
                 nc.tensor.matmul_mx(
@@ -184,16 +187,19 @@ def tile_quantumneuralnetwork_pa_t_kernel(tc, h0, w1, b1, q1_qw, q1_cw, q1_cb, o
                     stop=True,
                 )
                 nc.scalar.activation(
-                    out=h1_planes[:, t, :], in_=product1[:], func=ACT.Relu, bias=b1_column[:, t : t + 1], scale=1.0
+                    out=h1_planes[g][:, t, :], in_=product1[:], func=ACT.Relu, bias=b1_column[:, t : t + 1], scale=1.0
                 )
-            h1_grouped = work.tile([P, ROWS, PACK], BF16, name="h1_grouped", align_bytes=64)
-            nc.vector.tensor_copy(
-                out=h1_grouped[:].rearrange("q (c i) t -> q c t i", i=4),
-                in_=h1_planes[:].rearrange("q t (c i) -> q c t i", i=4),
-            )
-            h1_words, h1_scales = quantise(nc, work, h1_grouped[:].rearrange("q c t -> q (c t)"), "h1")
 
-            y = rows_out.tile([P, SUB, H], F32, name="y")
+        def regroup_h1(g):
+            h1_grouped[g] = work.tile([P, ROWS, PACK], BF16, name="h1_grouped", align_bytes=64)
+            nc.vector.tensor_copy(
+                out=h1_grouped[g][:].rearrange("q (c i) t -> q c t i", i=4),
+                in_=h1_planes[g][:].rearrange("q t (c i) -> q c t i", i=4),
+            )
+
+        def second_product(g):
+            h1_words, h1_scales = h1_packed[g]
+            results[g] = rows_out.tile([P, SUB, H], F32, name="y")
             for r in range(SUB):
                 product2 = psum_2.tile([P, H], F32, name="product2")
                 nc.tensor.matmul_mx(
@@ -205,6 +211,50 @@ def tile_quantumneuralnetwork_pa_t_kernel(tc, h0, w1, b1, q1_qw, q1_cw, q1_cb, o
                     start=True,
                     stop=True,
                 )
-                nc.vector.tensor_tensor(out=y[:, r, :], in0=product2[:], in1=bias_row[:], op=ALU.add)
-            nc.scalar.activation(out=y[:], in_=y[:], func=ACT.Tanh)
-            nc.sync.dma_start(out=out_rounds[g], in_=y[:])
+                nc.vector.tensor_tensor(out=results[g][:, r, :], in0=product2[:], in1=bias_row[:], op=ALU.add)
+
+        def tanh_and_store(g):
+            nc.scalar.activation(out=results[g][:], in_=results[g][:], func=ACT.Tanh)
+            nc.sync.dma_start(out=out_rounds[g], in_=results[g][:])
+
+        def pipeline_step(step):
+            def due(lag):
+                return 0 <= step - lag < ROUNDS
+
+            if due(SECOND_LAG):
+                second_product(step - SECOND_LAG)
+            if due(TANH_LAG):
+                tanh_and_store(step - TANH_LAG)
+            if due(0):
+                transpose_rows(step)
+            if due(REGROUP_LAG):
+                regroup_h1(step - REGROUP_LAG)
+            if due(FIRST_LAG):
+                first_product(step - FIRST_LAG)
+            if due(0):
+                h0_packed[step] = quantise(nc, work, h0_grouped[step][:], "h0")
+            if due(REGROUP_LAG):
+                g = step - REGROUP_LAG
+                h1_packed[g] = quantise(nc, work, h1_grouped[g][:].rearrange("q c t -> q (c t)"), "h1")
+
+        pipeline_step(0)
+        cw_grouped = keep.tile([P, H, PACK], BF16, name="cw_grouped", align_bytes=64)
+        nc.vector.tensor_copy(out=cw_grouped[:], in_=cw_raw[:].rearrange("q t n -> q n t"))
+        cw_words, cw_scales = quantise(nc, keep, cw_grouped[:].rearrange("q n t -> q (n t)"), "cw")
+        for step in range(1, SECOND_LAG):
+            pipeline_step(step)
+        spread = psum_2.tile([P, PACK, P], F32, name="spread", tag="product2")
+        for i in range(PACK):
+            nc.tensor.matmul(
+                out=spread[:, i, :],
+                lhsT=bias_column[:, i : i + 1].to_broadcast([P, P]),
+                rhs=ident[:],
+                start=True,
+                stop=True,
+            )
+        bias_row = keep.tile([P, H], F32, name="bias_row")
+        nc.vector.tensor_copy(
+            out=bias_row[:].rearrange("p (q i) -> p q i", i=PACK), in_=spread[:].rearrange("p i q -> p q i")
+        )
+        for step in range(SECOND_LAG, ROUNDS + TANH_LAG):
+            pipeline_step(step)

@@ -25,10 +25,11 @@ COS = 0
 SIN = 1
 THETA = 0
 PHI = 1
-FIRST_LAG = 1
-REGROUP_LAG = 2
-SECOND_LAG = 3
-TANH_LAG = 4
+COPY_LAG = 1
+FIRST_LAG = 2
+REGROUP_LAG = 3
+SECOND_LAG = 4
+TANH_LAG = 5
 
 FLOPS = 2 * 2 * BATCH * H * H
 
@@ -155,93 +156,107 @@ def tile_quantumneuralnetwork_pa_t_kernel(tc, h0, w1, b1, q1_qw, q1_cw, q1_cb, o
         )
         w1_words, w1_scales = quantise(nc, keep, w1_grouped[:].rearrange("q j k -> q (j k)"), "w1")
 
-        h0_grouped, h0_packed, h1_planes, h1_grouped, h1_packed, results = {}, {}, {}, {}, {}, {}
+        flipped, h0_grouped, h0_packed, h1_planes, h1_grouped, h1_packed, results = {}, {}, {}, {}, {}, {}, {}
 
         def transpose_rows(g):
             x_words = x_tiles[g][:].bitcast(F32)
-            h0_grouped[g] = work.tile([P, ROWS * PACK], BF16, name="h0_grouped", align_bytes=64)
-            h0_pairs = h0_grouped[g][:].bitcast(F32).rearrange("q (h r c u) -> q h r c u", h=2, r=2, u=2)
             for half in range(2):
-                flipped = psum_t.tile([P, 2, 2, P], F32, name="flipped")
+                flipped[g, half] = psum_t.tile([P, 2, 2, P], F32, name="flipped")
                 for r in range(2):
                     for u in range(2):
                         square = ((2 * half + r) * 2 + u) * P
                         nc.tensor.transpose(
-                            out=flipped[:, r, u, :], in_=x_words[:, square : square + P], identity=ident[:]
+                            out=flipped[g, half][:, r, u, :], in_=x_words[:, square : square + P], identity=ident[:]
                         )
-                empty = nc.scalar.copy if half == 0 else nc.vector.tensor_copy
-                empty(out=h0_pairs[:, half], in_=flipped[:].rearrange("q r u c -> q r c u"))
 
-        def first_product(g):
+        def empty_bank(g, half):
+            if half == 0:
+                h0_grouped[g] = work.tile([P, ROWS * PACK], BF16, name="h0_grouped", align_bytes=64)
+            h0_pairs = h0_grouped[g][:].bitcast(F32).rearrange("q (h r c u) -> q h r c u", h=2, r=2, u=2)
+            nc.vector.tensor_copy(out=h0_pairs[:, half], in_=flipped[g, half][:].rearrange("q r u c -> q r c u"))
+
+        def quantise_h0(g):
+            h0_packed[g] = quantise(nc, work, h0_grouped[g][:], "h0")
+
+        def first_product(g, t):
             h0_words, h0_scales = h0_packed[g]
-            h1_planes[g] = work.tile([P, PACK, ROWS], BF16, name="h1_planes")
-            for t in range(PACK):
-                product1 = psum_1.tile([P, ROWS], F32, name="product1")
-                nc.tensor.matmul_mx(
-                    out=product1[:],
-                    lhsT=w1_words[:, t * P : (t + 1) * P].bitcast(FP8X4),
-                    lhsT_scale=w1_scales[:, t * P : (t + 1) * P],
-                    rhs=h0_words[:].bitcast(FP8X4),
-                    rhs_scale=h0_scales[:],
-                    start=True,
-                    stop=True,
-                )
-                nc.scalar.activation(
-                    out=h1_planes[g][:, t, :], in_=product1[:], func=ACT.Relu, bias=b1_column[:, t : t + 1], scale=1.0
-                )
+            if t == 0:
+                h1_planes[g] = work.tile([P, PACK, ROWS], BF16, name="h1_planes")
+            product1 = psum_1.tile([P, ROWS], F32, name="product1")
+            nc.tensor.matmul_mx(
+                out=product1[:],
+                lhsT=w1_words[:, t * P : (t + 1) * P].bitcast(FP8X4),
+                lhsT_scale=w1_scales[:, t * P : (t + 1) * P],
+                rhs=h0_words[:].bitcast(FP8X4),
+                rhs_scale=h0_scales[:],
+                start=True,
+                stop=True,
+            )
+            nc.scalar.activation(
+                out=h1_planes[g][:, t, :], in_=product1[:], func=ACT.Relu, bias=b1_column[:, t : t + 1], scale=1.0
+            )
 
         def regroup_h1(g):
             h1_grouped[g] = work.tile([P, ROWS, PACK], BF16, name="h1_grouped", align_bytes=64)
-            nc.vector.tensor_copy(
+            nc.gpsimd.tensor_scalar(
                 out=h1_grouped[g][:].rearrange("q (c i) t -> q c t i", i=4),
-                in_=h1_planes[g][:].rearrange("q t (c i) -> q c t i", i=4),
+                in0=h1_planes[g][:].rearrange("q t (c i) -> q c t i", i=4),
+                scalar1=1.0,
+                scalar2=0.0,
+                op0=ALU.mult,
+                op1=ALU.add,
             )
 
-        def second_product(g):
+        def quantise_h1(g):
+            h1_packed[g] = quantise(nc, work, h1_grouped[g][:].rearrange("q c t -> q (c t)"), "h1")
+
+        def second_product(g, r):
             h1_words, h1_scales = h1_packed[g]
-            results[g] = rows_out.tile([P, SUB, H], F32, name="y")
-            for r in range(SUB):
-                product2 = psum_2.tile([P, H], F32, name="product2")
-                nc.tensor.matmul_mx(
-                    out=product2[:],
-                    lhsT=h1_words[:, r * P : (r + 1) * P].bitcast(FP8X4),
-                    lhsT_scale=h1_scales[:, r * P : (r + 1) * P],
-                    rhs=cw_words[:].bitcast(FP8X4),
-                    rhs_scale=cw_scales[:],
-                    start=True,
-                    stop=True,
-                )
-                nc.vector.tensor_tensor(out=results[g][:, r, :], in0=product2[:], in1=bias_row[:], op=ALU.add)
+            if r == 0:
+                results[g] = rows_out.tile([P, SUB, H], F32, name="y")
+            product2 = psum_2.tile([P, H], F32, name="product2")
+            nc.tensor.matmul_mx(
+                out=product2[:],
+                lhsT=h1_words[:, r * P : (r + 1) * P].bitcast(FP8X4),
+                lhsT_scale=h1_scales[:, r * P : (r + 1) * P],
+                rhs=cw_words[:].bitcast(FP8X4),
+                rhs_scale=cw_scales[:],
+                start=True,
+                stop=True,
+            )
+            nc.vector.tensor_tensor(out=results[g][:, r, :], in0=product2[:], in1=bias_row[:], op=ALU.add)
 
         def tanh_and_store(g):
             nc.scalar.activation(out=results[g][:], in_=results[g][:], func=ACT.Tanh)
             nc.sync.dma_start(out=out_rounds[g], in_=results[g][:])
 
         def pipeline_step(step):
-            def due(lag):
-                return 0 <= step - lag < ROUNDS
+            def at(lag, stage, *args):
+                if 0 <= step - lag < ROUNDS:
+                    stage(step - lag, *args)
 
-            if due(SECOND_LAG):
-                second_product(step - SECOND_LAG)
-            if due(TANH_LAG):
-                tanh_and_store(step - TANH_LAG)
-            if due(0):
-                transpose_rows(step)
-            if due(REGROUP_LAG):
-                regroup_h1(step - REGROUP_LAG)
-            if due(FIRST_LAG):
-                first_product(step - FIRST_LAG)
-            if due(0):
-                h0_packed[step] = quantise(nc, work, h0_grouped[step][:], "h0")
-            if due(REGROUP_LAG):
-                g = step - REGROUP_LAG
-                h1_packed[g] = quantise(nc, work, h1_grouped[g][:].rearrange("q c t -> q (c t)"), "h1")
+            at(REGROUP_LAG, regroup_h1)
+            at(TANH_LAG, tanh_and_store)
+            at(SECOND_LAG, second_product, 0)
+            at(FIRST_LAG, first_product, 0)
+            at(COPY_LAG, empty_bank, 0)
+            at(SECOND_LAG, second_product, 1)
+            at(FIRST_LAG, first_product, 1)
+            at(COPY_LAG, empty_bank, 1)
+            at(SECOND_LAG, second_product, 2)
+            at(FIRST_LAG, first_product, 2)
+            at(REGROUP_LAG, quantise_h1)
+            at(SECOND_LAG, second_product, 3)
+            at(FIRST_LAG, first_product, 3)
+            at(COPY_LAG, quantise_h0)
+            at(0, transpose_rows)
 
-        pipeline_step(0)
+        for step in range(FIRST_LAG):
+            pipeline_step(step)
         cw_grouped = keep.tile([P, H, PACK], BF16, name="cw_grouped", align_bytes=64)
         nc.vector.tensor_copy(out=cw_grouped[:], in_=cw_raw[:].rearrange("q t n -> q n t"))
         cw_words, cw_scales = quantise(nc, keep, cw_grouped[:].rearrange("q n t -> q (n t)"), "cw")
-        for step in range(1, SECOND_LAG):
+        for step in range(FIRST_LAG, SECOND_LAG):
             pipeline_step(step)
         spread = psum_2.tile([P, PACK, P], F32, name="spread", tag="product2")
         for i in range(PACK):

@@ -169,11 +169,11 @@ def tile_quantumneuralnetwork_pa_t_kernel(tc, h0, w1, b1, q1_qw, q1_cw, q1_cb, o
                             out=flipped[g, half][:, r, u, :], in_=x_words[:, square : square + P], identity=ident[:]
                         )
 
-        def empty_bank(g, half):
+        def empty_bank(g, half, copy):
             if half == 0:
                 h0_grouped[g] = work.tile([P, ROWS * PACK], BF16, name="h0_grouped", align_bytes=64)
             h0_pairs = h0_grouped[g][:].bitcast(F32).rearrange("q (h r c u) -> q h r c u", h=2, r=2, u=2)
-            nc.vector.tensor_copy(out=h0_pairs[:, half], in_=flipped[g, half][:].rearrange("q r u c -> q r c u"))
+            copy(out=h0_pairs[:, half], in_=flipped[g, half][:].rearrange("q r u c -> q r c u"))
 
         def quantise_h0(g):
             h0_packed[g] = quantise(nc, work, h0_grouped[g][:], "h0")
@@ -198,13 +198,9 @@ def tile_quantumneuralnetwork_pa_t_kernel(tc, h0, w1, b1, q1_qw, q1_cw, q1_cb, o
 
         def regroup_h1(g):
             h1_grouped[g] = work.tile([P, ROWS, PACK], BF16, name="h1_grouped", align_bytes=64)
-            nc.gpsimd.tensor_scalar(
+            nc.vector.tensor_copy(
                 out=h1_grouped[g][:].rearrange("q (c i) t -> q c t i", i=4),
-                in0=h1_planes[g][:].rearrange("q t (c i) -> q c t i", i=4),
-                scalar1=1.0,
-                scalar2=0.0,
-                op0=ALU.mult,
-                op1=ALU.add,
+                in_=h1_planes[g][:].rearrange("q t (c i) -> q c t i", i=4),
             )
 
         def quantise_h1(g):
@@ -235,14 +231,14 @@ def tile_quantumneuralnetwork_pa_t_kernel(tc, h0, w1, b1, q1_qw, q1_cw, q1_cb, o
                 if 0 <= step - lag < ROUNDS:
                     stage(step - lag, *args)
 
-            at(REGROUP_LAG, regroup_h1)
+            at(COPY_LAG, empty_bank, 0, nc.scalar.copy)
             at(TANH_LAG, tanh_and_store)
             at(SECOND_LAG, second_product, 0)
             at(FIRST_LAG, first_product, 0)
-            at(COPY_LAG, empty_bank, 0)
+            at(REGROUP_LAG, regroup_h1)
             at(SECOND_LAG, second_product, 1)
             at(FIRST_LAG, first_product, 1)
-            at(COPY_LAG, empty_bank, 1)
+            at(COPY_LAG, empty_bank, 1, nc.vector.tensor_copy)
             at(SECOND_LAG, second_product, 2)
             at(FIRST_LAG, first_product, 2)
             at(REGROUP_LAG, quantise_h1)

@@ -29,7 +29,6 @@ COPY_LAG = 1
 FIRST_LAG = 2
 REGROUP_LAG = 3
 SECOND_LAG = 4
-TANH_LAG = 5
 
 FLOPS = 2 * 2 * BATCH * H * H
 
@@ -118,6 +117,7 @@ def tile_quantumneuralnetwork_pa_t_kernel(tc, h0, w1, b1, q1_qw, q1_cw, q1_cb, o
         small = ctx.enter_context(tc.tile_pool(name="small", bufs=2))
         rows_in = ctx.enter_context(tc.tile_pool(name="rows_in", bufs=ROUNDS))
         work = ctx.enter_context(tc.tile_pool(name="work", bufs=3))
+        single = ctx.enter_context(tc.tile_pool(name="single", bufs=1))
         rows_out = ctx.enter_context(tc.tile_pool(name="rows_out", bufs=4))
         psum_t = ctx.enter_context(tc.psum_pool(name="psum_t", bufs=2))
         psum_1 = ctx.enter_context(tc.psum_pool(name="psum_1", bufs=3))
@@ -169,11 +169,11 @@ def tile_quantumneuralnetwork_pa_t_kernel(tc, h0, w1, b1, q1_qw, q1_cw, q1_cb, o
                             out=flipped[g, half][:, r, u, :], in_=x_words[:, square : square + P], identity=ident[:]
                         )
 
-        def empty_bank(g, half, copy):
+        def empty_bank(g, half):
             if half == 0:
                 h0_grouped[g] = work.tile([P, ROWS * PACK], BF16, name="h0_grouped", align_bytes=64)
             h0_pairs = h0_grouped[g][:].bitcast(F32).rearrange("q (h r c u) -> q h r c u", h=2, r=2, u=2)
-            copy(out=h0_pairs[:, half], in_=flipped[g, half][:].rearrange("q r u c -> q r c u"))
+            nc.vector.tensor_copy(out=h0_pairs[:, half], in_=flipped[g, half][:].rearrange("q r u c -> q r c u"))
 
         def quantise_h0(g):
             h0_packed[g] = quantise(nc, work, h0_grouped[g][:], "h0")
@@ -197,10 +197,14 @@ def tile_quantumneuralnetwork_pa_t_kernel(tc, h0, w1, b1, q1_qw, q1_cw, q1_cb, o
             )
 
         def regroup_h1(g):
-            h1_grouped[g] = work.tile([P, ROWS, PACK], BF16, name="h1_grouped", align_bytes=64)
-            nc.vector.tensor_copy(
+            h1_grouped[g] = single.tile([P, ROWS, PACK], BF16, name="h1_grouped", align_bytes=64)
+            nc.gpsimd.tensor_scalar(
                 out=h1_grouped[g][:].rearrange("q (c i) t -> q c t i", i=4),
-                in_=h1_planes[g][:].rearrange("q t (c i) -> q c t i", i=4),
+                in0=h1_planes[g][:].rearrange("q t (c i) -> q c t i", i=4),
+                scalar1=1.0,
+                scalar2=0.0,
+                op0=ALU.mult,
+                op1=ALU.add,
             )
 
         def quantise_h1(g):
@@ -222,38 +226,35 @@ def tile_quantumneuralnetwork_pa_t_kernel(tc, h0, w1, b1, q1_qw, q1_cw, q1_cb, o
             )
             nc.vector.tensor_tensor(out=results[g][:, r, :], in0=product2[:], in1=bias_row[:], op=ALU.add)
 
-        def tanh_and_store(g):
-            nc.scalar.activation(out=results[g][:], in_=results[g][:], func=ACT.Tanh)
-            nc.sync.dma_start(out=out_rounds[g], in_=results[g][:])
+        def tanh_and_store(g, r):
+            nc.scalar.activation(out=results[g][:, r, :], in_=results[g][:, r, :], func=ACT.Tanh)
+            nc.sync.dma_start(out=out_rounds[g][:, r, :], in_=results[g][:, r, :])
 
         def pipeline_step(step):
             def at(lag, stage, *args):
                 if 0 <= step - lag < ROUNDS:
                     stage(step - lag, *args)
 
-            at(COPY_LAG, empty_bank, 0, nc.scalar.copy)
-            at(TANH_LAG, tanh_and_store)
-            at(SECOND_LAG, second_product, 0)
-            at(FIRST_LAG, first_product, 0)
+            at(SECOND_LAG, quantise_h1)
             at(REGROUP_LAG, regroup_h1)
-            at(SECOND_LAG, second_product, 1)
-            at(FIRST_LAG, first_product, 1)
-            at(COPY_LAG, empty_bank, 1, nc.vector.tensor_copy)
-            at(SECOND_LAG, second_product, 2)
-            at(FIRST_LAG, first_product, 2)
-            at(REGROUP_LAG, quantise_h1)
-            at(SECOND_LAG, second_product, 3)
-            at(FIRST_LAG, first_product, 3)
-            at(COPY_LAG, quantise_h0)
+            at(COPY_LAG, empty_bank, 0)
+            at(COPY_LAG, empty_bank, 1)
+            at(FIRST_LAG, first_product, 0)
+            for i in range(1, PACK):
+                at(FIRST_LAG, first_product, i)
+                at(SECOND_LAG, second_product, i - 1)
+            at(SECOND_LAG, second_product, SUB - 1)
+            for r in range(SUB):
+                at(SECOND_LAG, tanh_and_store, r)
             at(0, transpose_rows)
+            at(COPY_LAG, quantise_h0)
 
-        for step in range(FIRST_LAG):
+        for step in range(REGROUP_LAG):
             pipeline_step(step)
         cw_grouped = keep.tile([P, H, PACK], BF16, name="cw_grouped", align_bytes=64)
         nc.vector.tensor_copy(out=cw_grouped[:], in_=cw_raw[:].rearrange("q t n -> q n t"))
         cw_words, cw_scales = quantise(nc, keep, cw_grouped[:].rearrange("q n t -> q (n t)"), "cw")
-        for step in range(FIRST_LAG, SECOND_LAG):
-            pipeline_step(step)
+        pipeline_step(REGROUP_LAG)
         spread = psum_2.tile([P, PACK, P], F32, name="spread", tag="product2")
         for i in range(PACK):
             nc.tensor.matmul(
@@ -267,5 +268,5 @@ def tile_quantumneuralnetwork_pa_t_kernel(tc, h0, w1, b1, q1_qw, q1_cw, q1_cb, o
         nc.vector.tensor_copy(
             out=bias_row[:].rearrange("p (q i) -> p q i", i=PACK), in_=spread[:].rearrange("p i q -> p q i")
         )
-        for step in range(SECOND_LAG, ROUNDS + TANH_LAG):
+        for step in range(SECOND_LAG, ROUNDS + SECOND_LAG):
             pipeline_step(step)

@@ -117,7 +117,7 @@ def tile_quantumneuralnetwork_pa_t_kernel(tc, h0, w1, b1, q1_qw, q1_cw, q1_cb, o
         small = ctx.enter_context(tc.tile_pool(name="small", bufs=2))
         rows_in = ctx.enter_context(tc.tile_pool(name="rows_in", bufs=ROUNDS))
         work = ctx.enter_context(tc.tile_pool(name="work", bufs=3))
-        single = ctx.enter_context(tc.tile_pool(name="single", bufs=1))
+        single = ctx.enter_context(tc.tile_pool(name="single", bufs=3))
         rows_out = ctx.enter_context(tc.tile_pool(name="rows_out", bufs=4))
         psum_t = ctx.enter_context(tc.psum_pool(name="psum_t", bufs=2))
         psum_1 = ctx.enter_context(tc.psum_pool(name="psum_1", bufs=3))

import math
from contextlib import ExitStack

import concourse.mybir as mybir
from concourse.masks import make_identity

F32 = mybir.dt.float32
BF16 = mybir.dt.bfloat16
U32 = mybir.dt.uint32
U8 = mybir.dt.uint8
FP8X4 = mybir.dt.float8_e4m3fn_x4
ACT = mybir.ActivationFunctionType
ALU = mybir.AluOpType

P = 128
PACK = 4
BATCH = 8192
H = P * PACK
DEPTH = 3
ROWS = 512
SUB = ROWS // P
ROUNDS = BATCH // ROWS
ROUND_TO_INT = 1.5 * 2.0**23
COS = 0
SIN = 1
THETA = 0
PHI = 1
COPY_LAG = 1
FIRST_LAG = 2
REGROUP_LAG = 3
SECOND_LAG = 4

FLOPS = 2 * 2 * BATCH * H * H


def quantise(nc, pool, grouped, name):
    columns = grouped.shape[1] // PACK
    words = pool.tile([P, columns], U32, name=name + "_words", align_bytes=64)
    scales = pool.tile([P, columns], U8, name=name + "_scales", align_bytes=64)
    nc.vector.quantize_mx(out=words[:].bitcast(FP8X4), scales=scales[:], in_=grouped)
    return words, scales


def output_bias_column(nc, small, q1_qw, q1_cb):
    angles = small.tile([P, DEPTH, PACK * 4], BF16, name="angles")
    nc.scalar.dma_start(out=angles[:], in_=q1_qw.rearrange("d (q i) a b -> q d (i a b)", i=PACK))
    cb = small.tile([P, PACK], BF16, name="cb")
    nc.scalar.dma_start(out=cb[:], in_=q1_cb.rearrange("(q i) -> q i", i=PACK))

    diagonal = angles[:].rearrange("q d (i e) -> q (d i) e", e=4)[:, :, 0:4:3]
    turns = small.tile([P, 2, DEPTH * PACK, 2], F32, name="turns")
    nc.vector.tensor_scalar(
        out=turns[:, COS], in0=diagonal, scalar1=0.5 / math.pi, scalar2=0.25, op0=ALU.mult, op1=ALU.add
    )
    nc.vector.tensor_scalar(
        out=turns[:, SIN], in0=diagonal, scalar1=0.5 / math.pi, scalar2=0.0, op0=ALU.mult, op1=ALU.add
    )
    whole = small.tile([P, 2, DEPTH * PACK, 2], F32, name="whole")
    nc.vector.tensor_scalar(
        out=whole[:], in0=turns[:], scalar1=ROUND_TO_INT, scalar2=ROUND_TO_INT, op0=ALU.add, op1=ALU.subtract
    )
    part = small.tile([P, 2, DEPTH * PACK, 2], F32, name="part")
    nc.vector.tensor_tensor(out=part[:], in0=turns[:], in1=whole[:], op=ALU.subtract)
    trig = small.tile([P, 2, DEPTH * PACK, 2], F32, name="trig")
    nc.scalar.activation(out=trig[:], in_=part[:], func=ACT.Sin, scale=2.0 * math.pi)

    def layer(d):
        return slice(d * PACK, (d + 1) * PACK)

    def rotation(kind, d):
        return trig[:, kind, layer(d), THETA].unsqueeze(1).to_broadcast([P, 2, PACK])

    a0 = small.tile([P, 2, PACK], F32, name="a0_first")
    nc.gpsimd.memset(a0[:, 1, :], 0.0)
    nc.gpsimd.tensor_copy(out=a0[:, 0, :], in_=trig[:, COS, layer(0), THETA])
    a1 = small.tile([P, 2, PACK], F32, name="a1_first")
    nc.gpsimd.tensor_tensor(out=a1[:], in0=trig[:, :, layer(0), PHI], in1=rotation(SIN, 0), op=ALU.mult)
    for d in range(1, DEPTH):
        cos_a0 = small.tile([P, 2, PACK], F32)
        sin_a1 = small.tile([P, 2, PACK], F32)
        new_a0 = small.tile([P, 2, PACK], F32)
        nc.gpsimd.tensor_tensor(out=cos_a0[:], in0=a0[:], in1=rotation(COS, d), op=ALU.mult)
        nc.gpsimd.tensor_tensor(out=sin_a1[:], in0=a1[:], in1=rotation(SIN, d), op=ALU.mult)
        nc.gpsimd.tensor_tensor(out=new_a0[:], in0=cos_a0[:], in1=sin_a1[:], op=ALU.subtract)
        if d < DEPTH - 1:
            sin_a0 = small.tile([P, 2, PACK], F32)
            cos_a1 = small.tile([P, 2, PACK], F32)
            turned = small.tile([P, 2, PACK], F32)
            nc.gpsimd.tensor_tensor(out=sin_a0[:], in0=a0[:], in1=rotation(SIN, d), op=ALU.mult)
            nc.gpsimd.tensor_tensor(out=cos_a1[:], in0=a1[:], in1=rotation(COS, d), op=ALU.mult)
            nc.gpsimd.tensor_tensor(out=turned[:], in0=sin_a0[:], in1=cos_a1[:], op=ALU.add)
            by_cos = small.tile([P, 2, PACK], F32)
            by_sin = small.tile([P, 2, PACK], F32)
            new_a1 = small.tile([P, 2, PACK], F32)
            cos_phi = trig[:, COS, layer(d), PHI].unsqueeze(1).to_broadcast([P, 2, PACK])
            sin_phi = trig[:, SIN, layer(d), PHI].unsqueeze(1).to_broadcast([P, 2, PACK])
            nc.gpsimd.tensor_tensor(out=by_cos[:], in0=turned[:], in1=cos_phi, op=ALU.mult)
            nc.gpsimd.tensor_tensor(out=by_sin[:], in0=turned[:], in1=sin_phi, op=ALU.mult)
            nc.gpsimd.tensor_tensor(out=new_a1[:, 0, :], in0=by_cos[:, 0, :], in1=by_sin[:, 1, :], op=ALU.subtract)
            nc.gpsimd.tensor_tensor(out=new_a1[:, 1, :], in0=by_sin[:, 0, :], in1=by_cos[:, 1, :], op=ALU.add)
            a1 = new_a1
        a0 = new_a0
    squares = small.tile([P, 2, PACK], F32, name="squares")
    nc.gpsimd.tensor_tensor(out=squares[:], in0=a0[:], in1=a0[:], op=ALU.mult)
    prob = small.tile([P, PACK], F32, name="prob")
    nc.gpsimd.tensor_tensor(out=prob[:], in0=squares[:, 0, :], in1=squares[:, 1, :], op=ALU.add)
    bias_column = small.tile([P, PACK], F32, name="bias_column")
    nc.gpsimd.tensor_tensor(out=bias_column[:], in0=prob[:], in1=cb[:], op=ALU.add)
    return bias_column


def tile_quantumneuralnetwork_pa_t_kernel(tc, h0, w1, b1, q1_qw, q1_cw, q1_cb, out):
    nc = tc.nc
    with ExitStack() as ctx:
        ctx.enter_context(tc.manual_schedule())
        keep = ctx.enter_context(tc.tile_pool(name="keep", bufs=1))
        small = ctx.enter_context(tc.tile_pool(name="small", bufs=2))
        rows_in = ctx.enter_context(tc.tile_pool(name="rows_in", bufs=ROUNDS))
        work = ctx.enter_context(tc.tile_pool(name="work", bufs=3))
        single = ctx.enter_context(tc.tile_pool(name="single", bufs=3))
        rows_out = ctx.enter_context(tc.tile_pool(name="rows_out", bufs=4))
        psum_t = ctx.enter_context(tc.psum_pool(name="psum_t", bufs=2))
        psum_1 = ctx.enter_context(tc.psum_pool(name="psum_1", bufs=3))
        psum_2 = ctx.enter_context(tc.psum_pool(name="psum_2", bufs=3))

        h0_rounds = h0.rearrange("(g c r) k -> g c (r k)", c=P, r=SUB)
        out_rounds = out.rearrange("(g c r) n -> g c r n", c=P, r=SUB)

        w1_raw = keep.tile([P, PACK, H], BF16, name="w1_raw")
        nc.sync.dma_start(
            out=w1_raw[:].rearrange("q (u e) j -> q u e j", u=2),
            in_=w1.rearrange("(u q e) j -> q u e j", u=2, e=2),
        )
        x_tiles = []
        for g in range(ROUNDS):
            x_tiles.append(rows_in.tile([P, SUB * H], BF16, name="x"))
        nc.sync.dma_start(out=x_tiles[0][:], in_=h0_rounds[0])
        nc.sync.dma_start(out=x_tiles[1][:], in_=h0_rounds[1])
        cw_raw = keep.tile([P, PACK, H], BF16, name="cw_raw")
        nc.sync.dma_start(out=cw_raw[:], in_=q1_cw.rearrange("(q t) n -> q t n", t=PACK))
        for g in range(2, ROUNDS):
            nc.sync.dma_start(out=x_tiles[g][:], in_=h0_rounds[g])

        ident = keep.tile([P, P], F32, name="ident")
        make_identity(nc, ident[:])
        b1_raw = small.tile([P, PACK], BF16, name="b1_raw")
        nc.scalar.dma_start(out=b1_raw[:], in_=b1.rearrange("(q t) -> q t", t=PACK))
        bias_column = output_bias_column(nc, small, q1_qw, q1_cb)
        b1_column = keep.tile([P, PACK], F32, name="b1_column")
        nc.vector.tensor_copy(out=b1_column[:], in_=b1_raw[:])

        w1_grouped = keep.tile([P, H, PACK], BF16, name="w1_grouped", align_bytes=64)
        nc.vector.tensor_copy(
            out=w1_grouped[:].rearrange("q (t m) k -> q t m k", t=PACK),
            in_=w1_raw[:].rearrange("q k (m t) -> q t m k", t=PACK),
        )
        w1_words, w1_scales = quantise(nc, keep, w1_grouped[:].rearrange("q j k -> q (j k)"), "w1")

        flipped, h0_grouped, h0_packed, h1_planes, h1_grouped, h1_packed, results = {}, {}, {}, {}, {}, {}, {}

        def transpose_rows(g):
            x_words = x_tiles[g][:].bitcast(F32)
            for half in range(2):
                flipped[g, half] = psum_t.tile([P, 2, 2, P], F32, name="flipped")
                for r in range(2):
                    for u in range(2):
                        square = ((2 * half + r) * 2 + u) * P
                        nc.tensor.transpose(
                            out=flipped[g, half][:, r, u, :], in_=x_words[:, square : square + P], identity=ident[:]
                        )

        def empty_bank(g, half):
            if half == 0:
                h0_grouped[g] = work.tile([P, ROWS * PACK], BF16, name="h0_grouped", align_bytes=64)
            h0_pairs = h0_grouped[g][:].bitcast(F32).rearrange("q (h r c u) -> q h r c u", h=2, r=2, u=2)
            nc.vector.tensor_copy(out=h0_pairs[:, half], in_=flipped[g, half][:].rearrange("q r u c -> q r c u"))

        def quantise_h0(g):
            h0_packed[g] = quantise(nc, work, h0_grouped[g][:], "h0")

        def first_product(g, t):
            h0_words, h0_scales = h0_packed[g]
            if t == 0:
                h1_planes[g] = work.tile([P, PACK, ROWS], BF16, name="h1_planes")
            product1 = psum_1.tile([P, ROWS], F32, name="product1")
            nc.tensor.matmul_mx(
                out=product1[:],
                lhsT=w1_words[:, t * P : (t + 1) * P].bitcast(FP8X4),
                lhsT_scale=w1_scales[:, t * P : (t + 1) * P],
                rhs=h0_words[:].bitcast(FP8X4),
                rhs_scale=h0_scales[:],
                start=True,
                stop=True,
            )
            nc.scalar.activation(
                out=h1_planes[g][:, t, :], in_=product1[:], func=ACT.Relu, bias=b1_column[:, t : t + 1], scale=1.0
            )

        def regroup_h1(g):
            h1_grouped[g] = single.tile([P, ROWS, PACK], BF16, name="h1_grouped", align_bytes=64)
            nc.gpsimd.tensor_scalar(
                out=h1_grouped[g][:].rearrange("q (c i) t -> q c t i", i=4),
                in0=h1_planes[g][:].rearrange("q t (c i) -> q c t i", i=4),
                scalar1=1.0,
                scalar2=0.0,
                op0=ALU.mult,
                op1=ALU.add,
            )

        def quantise_h1(g):
            h1_packed[g] = quantise(nc, work, h1_grouped[g][:].rearrange("q c t -> q (c t)"), "h1")

        def second_product(g, r):
            h1_words, h1_scales = h1_packed[g]
            if r == 0:
                results[g] = rows_out.tile([P, SUB, H], F32, name="y")
            product2 = psum_2.tile([P, H], F32, name="product2")
            nc.tensor.matmul_mx(
                out=product2[:],
                lhsT=h1_words[:, r * P : (r + 1) * P].bitcast(FP8X4),
                lhsT_scale=h1_scales[:, r * P : (r + 1) * P],
                rhs=cw_words[:].bitcast(FP8X4),
                rhs_scale=cw_scales[:],
                start=True,
                stop=True,
            )
            nc.vector.tensor_tensor(out=results[g][:, r, :], in0=product2[:], in1=bias_row[:], op=ALU.add)

        def tanh_and_store(g, r):
            nc.scalar.activation(out=results[g][:, r, :], in_=results[g][:, r, :], func=ACT.Tanh)
            nc.sync.dma_start(out=out_rounds[g][:, r, :], in_=results[g][:, r, :])

        def pipeline_step(step):
            def at(lag, stage, *args):
                if 0 <= step - lag < ROUNDS:
                    stage(step - lag, *args)

            at(SECOND_LAG, quantise_h1)
            at(REGROUP_LAG, regroup_h1)
            at(COPY_LAG, empty_bank, 0)
            at(COPY_LAG, empty_bank, 1)
            at(FIRST_LAG, first_product, 0)
            for i in range(1, PACK):
                at(FIRST_LAG, first_product, i)
                at(SECOND_LAG, second_product, i - 1)
            at(SECOND_LAG, second_product, SUB - 1)
            for r in range(SUB):
                at(SECOND_LAG, tanh_and_store, r)
            at(0, transpose_rows)
            at(COPY_LAG, quantise_h0)

        for step in range(REGROUP_LAG):
            pipeline_step(step)
        cw_grouped = keep.tile([P, H, PACK], BF16, name="cw_grouped", align_bytes=64)
        nc.vector.tensor_copy(out=cw_grouped[:], in_=cw_raw[:].rearrange("q t n -> q n t"))
        cw_words, cw_scales = quantise(nc, keep, cw_grouped[:].rearrange("q n t -> q (n t)"), "cw")
        pipeline_step(REGROUP_LAG)
        spread = psum_2.tile([P, PACK, P], F32, name="spread", tag="product2")
        for i in range(PACK):
            nc.tensor.matmul(
                out=spread[:, i, :],
                lhsT=bias_column[:, i : i + 1].to_broadcast([P, P]),
                rhs=ident[:],
                start=True,
                stop=True,
            )
        bias_row = keep.tile([P, H], F32, name="bias_row")
        nc.vector.tensor_copy(
            out=bias_row[:].rearrange("p (q i) -> p q i", i=PACK), in_=spread[:].rearrange("p i q -> p q i")
        )
        for step in range(SECOND_LAG, ROUNDS + SECOND_LAG):
            pipeline_step(step)
